import numpy as np
import ml_dtypes


def mxq(x, axis, fmt="e4m3"):
    dtype, down = {"e4m3": (ml_dtypes.float8_e4m3fn, 7), "e5m2": (ml_dtypes.float8_e5m2, 14)}[fmt]
    v = np.moveaxis(np.asarray(x, np.float32).astype(ml_dtypes.bfloat16).astype(np.float64), axis, -1)
    blocks = v.reshape(v.shape[:-1] + (-1, 32))
    amax = np.abs(blocks).max(-1, keepdims=True)
    byte = np.maximum(np.where(amax > 0, np.frexp(amax)[1] - 1 + 127, 0) - down, 1)
    scale = np.exp2(byte - 127.0)
    codes = (blocks / scale).astype(np.float32).astype(dtype).astype(np.float64)
    return np.moveaxis((codes * scale).reshape(v.shape), -1, axis)


WIDE = False


def mx_kscale(k):
    if not WIDE:
        return np.ones(k)
    levels = np.array([10, -10, 5, -5, 0])
    if k % 512:
        return np.exp2(np.random.permutation(np.resize(levels, k // 32))).repeat(32)
    a = np.empty((k // 512, 16))
    for p in range(k // 512):
        a[p, :8] = np.random.permutation(np.resize(levels, 8))
        for g in range(8):
            far = levels[np.abs(levels - a[p, g]) >= 10]
            a[p, g + 8] = far[np.random.randint(len(far))]
    return np.exp2(a.ravel()).repeat(32)


BF16 = ml_dtypes.bfloat16


def bf(x):
    return np.asarray(x, np.float32).astype(BF16)


def f64(x):
    return np.asarray(x).astype(np.float64)


B, N, C, O = 2, 512, 512, 512
G = 3 * C


def sigmoid(v):
    return 1.0 / (1.0 + np.exp(-v))


def gru_step(gx, h, gru_U, gru_b_h):
    gh = h @ gru_U + gru_b_h
    xz, xr, xh = np.split(gx, 3, axis=-1)
    hz, hr, hh = np.split(gh, 3, axis=-1)
    z = sigmoid(xz + hz)
    r = sigmoid(xr + hr)
    hcand = np.tanh(xh + r * hh)
    hnew = z * h + (1.0 - z) * hcand
    return np.concatenate([z, r, hcand], axis=-1), hh, hnew


def setup_inputs():
    s = mx_kscale(B * N).reshape(B, N, 1)
    u = mx_kscale(O)
    v = mx_kscale(C)
    v3 = np.concatenate([v, v, v])
    gx = bf(np.random.standard_normal((B * N, G)))
    a0 = bf(np.random.standard_normal((B, N, C)))
    U0 = bf(np.random.standard_normal((C, G)) / np.sqrt(C))
    gru_b_h = bf(np.random.standard_normal(G) * 0.3)
    W0 = bf(np.random.standard_normal((C, O)) * 1.5 / np.sqrt(C))
    dense_b = bf(np.random.standard_normal(O) * 0.1)
    g = bf(np.random.standard_normal((B, N, O)) * 4.0 * np.exp2(np.random.randint(-6, 1, (B, N, 1))) / s * u)
    gates, hh, hnew = gru_step(f64(gx), f64(a0).reshape(-1, C), f64(U0), f64(gru_b_h))
    return {"gx": gx,
            "annotations": bf(f64(a0) * s),
            "gru_U": bf(f64(U0) * v[:, None] / v3),
            "gru_b_h": gru_b_h,
            "dense_W": bf(f64(W0) * v[:, None] / u),
            "dense_b": dense_b,
            "gates": np.asarray(gates, np.float32),
            "hh": np.asarray(hh, np.float32),
            "hnew": np.asarray(hnew, np.float32),
            "grad_out": g}


def reference(gx, annotations, gru_U, gru_b_h, dense_W, dense_b, gates, hh, hnew, grad_out):
    h = f64(annotations).reshape(-1, C)
    g = f64(grad_out).reshape(-1, O)
    z, r, hcand = np.split(f64(gates), 3, axis=-1)
    hhf = f64(hh)
    hn = f64(hnew)
    dhnew = mxq(g, 1, "e5m2") @ mxq(f64(dense_W), 1, "e4m3").T
    dhz = dhnew * (hn - hcand) * (1.0 - z)
    dah = dhnew * (1.0 - z) * (1.0 - hcand * hcand)
    dhr = dah * hhf * r * (1.0 - r)
    dhh = dah * r
    dgh = np.concatenate([dhz, dhr, dhh], axis=-1)
    dh = (mxq(dgh, 1, "e5m2") @ mxq(f64(gru_U), 1, "e4m3").T) + dhnew * z
    dU = mxq(h, 0, "e4m3").T @ mxq(dgh, 0, "e5m2")
    return dh.reshape(B, N, C), dU

@@ -1,0 +1,393 @@
+from contextlib import ExitStack
+
+import concourse.mybir as mybir
+from concourse.masks import make_identity
+
+NODES, GROUP, C, O, G = 1024, 512, 512, 512, 1536
+P = 128
+FLOPS = 2 * NODES * C * O + 4 * NODES * C * G
+BYTES = 2 * (NODES * O + C * O + C * G + NODES * C) + 4 * (NODES * G + 2 * NODES * C) + 4 * (NODES * C + C * G)
+
+F32 = mybir.dt.float32
+BF16 = mybir.dt.bfloat16
+U32 = mybir.dt.uint32
+U8 = mybir.dt.uint8
+E4M3 = mybir.dt.float8_e4m3fn_x4
+E5M2 = mybir.dt.float8_e5m2_x4
+ADD = mybir.AluOpType.add
+SUB = mybir.AluOpType.subtract
+MULT = mybir.AluOpType.mult
+ACT = mybir.ActivationFunctionType
+Z, R, H = 0, 1, 2
+
+
+def tile_gatedgraphconvolution_pb_v_kernel(
+    tc, gx, annotations, gru_U, gru_b_h, dense_W, dense_b, gates, hh, hnew, grad_out, out_0, out_1
+):
+    nc = tc.nc
+    with ExitStack() as ctx:
+        pool = ctx.enter_context(tc.tile_pool(name="pool", bufs=1))
+        psum = ctx.enter_context(tc.psum_pool(name="psum", bufs=8))
+
+        def sb(shape, dtype, name, tag=None, bufs=1):
+            return pool.tile(shape, dtype, name=name, tag=tag or name, bufs=bufs, align_bytes=64)
+
+        def bank(name):
+            return psum.tile([P, 512], F32, name=name, tag="bank", bufs=8)
+
+        ident = sb([P, P], F32, "ident")
+        neg_half = sb([P, 1], F32, "neg_half")
+        warm = sb([P, 1], F32, "warm")
+
+        raw, fm, tm = {}, {}, {}
+        codes, scales = {}, {}
+        act = {}
+        banks = {}
+
+        def load_raw(name, src, pieces):
+            raw[name] = sb([P, 2048], BF16, "raw_" + name, "raw", 3)
+            n = 4 // pieces
+            view = raw[name][:].rearrange("p (j c) -> p j c", j=4)
+            for i in range(pieces):
+                nc.sync.dma_start(out=view[:, i * n : (i + 1) * n, :], in_=src[:, i * n : (i + 1) * n, :])
+
+        def load_act(name, g, src, pieces):
+            t = sb([P, 2048], F32, "%s%d" % (name, g))
+            act[name, g] = t
+            n = 4 // pieces
+            view = t[:].rearrange("p (j c) -> p j c", j=4)
+            for i in range(pieces):
+                nc.sync.dma_start(out=view[:, i * n : (i + 1) * n, :], in_=src[:, i * n : (i + 1) * n, :])
+
+        def gate_src(g, block):
+            return gates[GROUP * g : GROUP * (g + 1), 512 * block : 512 * (block + 1)].rearrange("(p j) c -> p j c", j=4)
+
+        def rows_src(x, g):
+            return x[GROUP * g : GROUP * (g + 1), :].rearrange("(p j) c -> p j c", j=4)
+
+        def turn(dst, words, base, u):
+            nc.tensor.transpose(dst, words[:, base + u : base + 256 : 2], ident[:])
+
+        def turn_rows(key, words, bases):
+            b = bank("tr_%s" % key)
+            banks[key] = b
+            for i, base in enumerate(bases):
+                for u in range(2):
+                    turn(b[:, 256 * i + 128 * u : 256 * i + 128 * (u + 1)], words, base, u)
+
+        def turn_gate(gate, g):
+            words = tm[gate, g][:].bitcast(F32)
+            for u in range(2):
+                b = bank("tf_%d_%d_%d" % (gate, g, u))
+                banks["f", gate, g, u] = b
+                for f in range(4):
+                    turn(b[:, 128 * f : 128 * (f + 1)], words, 256 * f, u)
+
+        def mx(out, lhs, lcols, lfmt, rhs, rfmt, start, stop):
+            nc.tensor.matmul_mx(
+                out=out[:],
+                lhsT=codes[lhs][:, lcols].bitcast(lfmt),
+                lhsT_scale=scales[lhs][:, lcols],
+                rhs=codes[rhs][:].bitcast(rfmt),
+                rhs_scale=scales[rhs][:],
+                start=start,
+                stop=stop,
+            )
+
+        def cols(i):
+            return slice(128 * i, 128 * (i + 1))
+
+        def mm_dhnew(g, j):
+            b = bank("dh_%d_%d" % (g, j))
+            banks["dh", g, j] = b
+            mx(b, ("g", g), cols(j), E5M2, "W", E4M3, True, True)
+
+        def mm_out0(g, j, parts, start, stop):
+            if start:
+                banks["o0", g, j] = bank("o0_%d_%d" % (g, j))
+            b = banks["o0", g, j]
+            for i, part in enumerate(parts):
+                st = start and i == 0
+                sp = stop and i == len(parts) - 1
+                if part == "dh":
+                    mx(b, ("g", g), cols(j), E5M2, "W", E4M3, st, sp)
+                else:
+                    mx(b, ("F", part, g), cols(j), E5M2, ("U", part), E4M3, st, sp)
+
+        def mm_out1(gate, m):
+            b = bank("o1_%d_%d" % (gate, m))
+            banks["o1", gate, m] = b
+            for g in range(2):
+                mx(b, ("h", g), cols(m), E4M3, ("T", gate, g), E5M2, g == 0, g == 1)
+
+        def feature_tile(key):
+            fm[key] = sb([P, 2048], BF16, "fm_%s" % "_".join(str(x) for x in (key if isinstance(key, tuple) else (key,))), "fm", 4)
+
+        def copy_rows(eng, key, half, bank_key):
+            out = fm[key][:].bitcast(F32)[:, 512 * half : 512 * (half + 1)].rearrange("q (m p u) -> q m p u", m=2, u=2)
+            in_ = banks[bank_key][:].rearrange("q (m u p) -> q m p u", m=2, u=2)
+            if eng == "s":
+                nc.scalar.copy(out=out, in_=in_)
+            else:
+                nc.vector.tensor_copy(out=out, in_=in_)
+
+        def copy_gate(eng, gate, g, u):
+            out = fm["F", gate, g][:, 1024 * u : 1024 * (u + 1)].rearrange("q (e p f) -> q e p f", e=2, f=4)
+            in_ = banks["f", gate, g, u][:].bitcast(BF16).rearrange("q (f p e) -> q e p f", f=4, e=2)
+            sign = -1.0 if gate == R else 1.0
+            if eng == "s":
+                nc.scalar.activation(out=out, in_=in_, func=ACT.Copy, scale=sign)
+            else:
+                nc.vector.tensor_scalar_mul(out, in_, sign)
+
+        def copy_out1(eng, gate, m):
+            stage = sb([P, 512], F32, "stage_%d_%d" % (gate, m), "stage", 4)
+            out = stage[:].rearrange("p (q f) -> p q f", f=4)
+            in_ = banks["o1", gate, m][:].rearrange("p (f q) -> p q f", f=4)
+            sign = -1.0 if gate == R else 1.0
+            if eng == "s":
+                nc.scalar.activation(out=out, in_=in_, func=ACT.Copy, scale=sign)
+            else:
+                nc.vector.tensor_scalar_mul(out, in_, sign)
+            nc.sync.dma_start(out=out_1[128 * m : 128 * (m + 1), 512 * gate : 512 * (gate + 1)], in_=stage[:])
+
+        def alloc_codes(key, tag, bufs):
+            nm = "_".join(str(x) for x in (key if isinstance(key, tuple) else (key,)))
+            codes[key] = sb([P, 512], U32, "c_" + nm, "c_" + tag, bufs)
+            scales[key] = sb([P, 512], U8, "s_" + nm, "s_" + tag, bufs)
+
+        def quant(key, src, fmt, tag, bufs, part=0, parts=1):
+            if part == 0:
+                alloc_codes(key, tag, bufs)
+            w = 512 // parts
+            c = slice(w * part, w * (part + 1))
+            nc.vector.quantize_mx(
+                out=codes[key][:, c].bitcast(fmt), scales=scales[key][:, c], in_=src[:, 4 * w * part : 4 * w * (part + 1)]
+            )
+
+        def vec_e(g, j):
+            if j == 0:
+                act["e", g] = sb([P, 2048], F32, "e%d" % g)
+            c = slice(512 * j, 512 * (j + 1))
+            nc.vector.scalar_tensor_tensor(
+                out=act["e", g][:, c].rearrange("p (q m) -> p q m", m=4),
+                in0=act["z", g][:, c].rearrange("p (q m) -> p q m", m=4),
+                scalar=1.0,
+                in1=banks["dh", g, j][:].rearrange("p (m q) -> p q m", m=4),
+                op0=SUB,
+                op1=MULT,
+            )
+
+        def scal_s(g, i, n):
+            if i == 0:
+                act["s", g] = sb([P, 2048], F32, "s%d" % g)
+            w = 2048 // n
+            c = slice(w * i, w * (i + 1))
+            nc.scalar.activation(out=act["s", g][:, c], in_=act["hc", g][:, c], func=ACT.Square)
+
+        def scal_sr(g, i, n):
+            if i == 0:
+                act["sr", g] = sb([P, 2048], F32, "sr%d" % g, "sr", 1)
+            w = 2048 // n
+            c = slice(w * i, w * (i + 1))
+            nc.scalar.activation(out=act["sr", g][:, c], in_=act["r", g][:, c], func=ACT.Square, bias=neg_half[:, 0:1])
+
+        def vec_dah(g, i, n):
+            w = 2048 // n
+            c = slice(w * i, w * (i + 1))
+            s = act["s", g]
+            nc.vector.scalar_tensor_tensor(out=s[:, c], in0=s[:, c], scalar=1.0, in1=act["e", g][:, c], op0=SUB, op1=MULT)
+
+        def vec_tp(g, i, n):
+            w = 2048 // n
+            c = slice(w * i, w * (i + 1))
+            hc = act["hc", g]
+            nc.vector.tensor_tensor(out=hc[:, c], in0=hc[:, c], in1=act["hn", g][:, c], op=SUB)
+
+        def vec_u2(g, i, n):
+            w = 2048 // n
+            c = slice(w * i, w * (i + 1))
+            hhg = act["hh", g]
+            nc.vector.scalar_tensor_tensor(out=hhg[:, c], in0=act["sr", g][:, c], scalar=0.25, in1=hhg[:, c], op0=SUB, op1=MULT)
+
+        def vec_gate(gate, g, a, b, i=0, n=1):
+            if i == 0:
+                tm[gate, g] = sb([P, 2048], BF16, "tm_%d_%d" % (gate, g), "tm", 4)
+            w = 128 // n
+            q = slice(w * i, w * (i + 1))
+            nc.vector.tensor_tensor(
+                out=tm[gate, g][:].rearrange("p (f q t) -> p q t f", f=4, t=4)[:, q, :, :],
+                in0=act[a, g][:].rearrange("p (t q f) -> p q t f", t=4, f=4)[:, q, :, :],
+                in1=act[b, g][:].rearrange("p (t q f) -> p q t f", t=4, f=4)[:, q, :, :],
+                op=MULT,
+            )
+
+        def vec_add(g, j):
+            c = slice(512 * j, 512 * (j + 1))
+            e = act["e", g]
+            nc.vector.tensor_tensor(
+                out=e[:, c].rearrange("p (q m) -> p q m", m=4),
+                in0=banks["o0", g, j][:].rearrange("p (m q) -> p q m", m=4),
+                in1=e[:, c].rearrange("p (q m) -> p q m", m=4),
+                op=ADD,
+            )
+            nc.sync.dma_start(out=out_0[g].rearrange("(p j) c -> p j c", j=4)[:, j, :], in_=e[:, c])
+
+        def interleave_h(g):
+            fm["h", g] = sb([P, 2048], BF16, "fm_h_%d" % g, "fm", 4)
+            nc.scalar.copy(
+                out=fm["h", g][:].rearrange("p (c i t) -> p c t i", i=4, t=4),
+                in_=raw["h%d" % g][:].rearrange("p (t c i) -> p c t i", t=4, i=4),
+            )
+
+        def q_t(gate, g):
+            quant(("T", gate, g), tm[gate, g], E5M2, "T%d%d" % (gate, g), 1)
+
+        def q_f(gate, g, part=0, parts=1):
+            quant(("F", gate, g), fm["F", gate, g], E5M2, "F", 4, part, parts)
+
+        with tc.manual_schedule():
+            load_raw("W", dense_W.rearrange("(p m) o -> p m o", m=4), 2)
+            load_raw("g0", grad_out[0].rearrange("(p j) o -> p j o", j=4), 2)
+            load_act("z", 0, gate_src(0, Z), 2)
+            load_act("hc", 0, gate_src(0, H), 2)
+            load_act("hn", 0, rows_src(hnew, 0), 2)
+            load_act("r", 0, gate_src(0, R), 1)
+            load_act("hh", 0, rows_src(hh, 0), 1)
+            load_raw("g1", grad_out[1].rearrange("(p j) o -> p j o", j=4), 1)
+            load_act("z", 1, gate_src(1, Z), 1)
+            load_act("hc", 1, gate_src(1, H), 1)
+            raw_u = sb([P, 4 * G], BF16, "raw_u")
+            u_src = gru_U.rearrange("(p m) k -> p (m k)", m=4)
+            for i in range(2):
+                nc.sync.dma_start(out=raw_u[:, 2 * G * i : 2 * G * (i + 1)], in_=u_src[:, 2 * G * i : 2 * G * (i + 1)])
+            load_act("hn", 1, rows_src(hnew, 1), 1)
+            load_act("r", 1, gate_src(1, R), 1)
+            load_act("hh", 1, rows_src(hh, 1), 1)
+            load_raw("h0", annotations[0].rearrange("(p j) c -> p j c", j=4), 1)
+            load_raw("h1", annotations[1].rearrange("(p j) c -> p j c", j=4), 1)
+
+            nc.vector.memset(neg_half[:], -0.5)
+            nc.vector.memset(warm[:], 0.0)
+            nc.scalar.activation(out=warm[:], in_=warm[:], func=ACT.Square)
+            make_identity(nc, ident[:])
+
+            w_words = raw["W"][:].bitcast(F32)
+            g0_words = raw["g0"][:].bitcast(F32)
+            feature_tile("W")
+            feature_tile(("g", 0))
+            for i in range(2):
+                turn_rows("W%d" % i, w_words, (512 * i, 512 * i + 256))
+            for i in range(2):
+                turn_rows("g0%d" % i, g0_words, (512 * i, 512 * i + 256))
+            copy_rows("s", "W", 0, "W0")
+            copy_rows("v", "W", 1, "W1")
+            copy_rows("s", ("g", 0), 0, "g00")
+            copy_rows("v", ("g", 0), 1, "g01")
+            quant("W", fm["W"], E4M3, "W", 1)
+            quant(("g", 0), fm["g", 0], E5M2, "g0", 1, 0, 2)
+            quant(("g", 0), fm["g", 0], E5M2, "g0", 1, 1, 2)
+            for j in range(4):
+                mm_dhnew(0, j)
+
+            scal_s(0, 0, 2)
+            scal_s(0, 1, 2)
+            for j in range(4):
+                vec_e(0, j)
+            vec_dah(0, 0, 2)
+            vec_dah(0, 1, 2)
+            scal_sr(0, 0, 1)
+            vec_tp(0, 0, 2)
+            vec_tp(0, 1, 2)
+            vec_gate(Z, 0, "e", "hc")
+            turn_gate(Z, 0)
+            feature_tile(("F", Z, 0))
+            copy_gate("s", Z, 0, 0)
+            copy_gate("s", Z, 0, 1)
+            vec_gate(H, 0, "s", "r")
+            feature_tile(("g", 1))
+            g1_words = raw["g1"][:].bitcast(F32)
+            for i in range(2):
+                turn_rows("g1%d" % i, g1_words, (512 * i, 512 * i + 256))
+                copy_rows("s", ("g", 1), i, "g1%d" % i)
+            q_t(Z, 0)
+            vec_u2(0, 0, 1)
+            turn_gate(H, 0)
+            feature_tile(("F", H, 0))
+            copy_gate("s", H, 0, 0)
+            copy_gate("s", H, 0, 1)
+            quant(("g", 1), fm["g", 1], E5M2, "g1", 1)
+            q_f(Z, 0)
+            for j in range(4):
+                mm_dhnew(1, j)
+            vec_gate(R, 0, "s", "hh")
+            scal_s(1, 0, 1)
+            q_t(H, 0)
+            for j in range(4):
+                vec_e(1, j)
+            q_f(H, 0)
+            q_t(R, 0)
+            turn_gate(R, 0)
+            feature_tile(("F", R, 0))
+            copy_gate("s", R, 0, 0)
+            copy_gate("s", R, 0, 1)
+            vec_dah(1, 0, 1)
+            u_words = raw_u[:].bitcast(F32)
+            for block in range(3):
+                feature_tile(("U", block))
+                for i in range(2):
+                    turn_rows(
+                        "U%d%d" % (block, i), u_words, (768 * 2 * i + 256 * block, 768 * (2 * i + 1) + 256 * block)
+                    )
+                    copy_rows("s", ("U", block), i, "U%d%d" % (block, i))
+            q_f(R, 0)
+            vec_tp(1, 0, 1)
+            for block in range(3):
+                quant(("U", block), fm["U", block], E4M3, "U%d" % block, 1)
+            scal_sr(1, 0, 1)
+            vec_gate(Z, 1, "e", "hc")
+            for j in range(4):
+                mm_out0(0, j, ("dh", Z, R, H), True, True)
+            for j in range(4):
+                vec_add(0, j)
+            turn_gate(Z, 1)
+            feature_tile(("F", Z, 1))
+            copy_gate("s", Z, 1, 0)
+            copy_gate("s", Z, 1, 1)
+            q_t(Z, 1)
+            interleave_h(0)
+            interleave_h(1)
+            vec_gate(H, 1, "s", "r")
+            turn_gate(H, 1)
+            q_f(Z, 1)
+            for g in range(2):
+                quant(("h", g), fm["h", g], E4M3, "h%d" % g, 1)
+            feature_tile(("F", H, 1))
+            copy_gate("s", H, 1, 0)
+            copy_gate("s", H, 1, 1)
+            for j in range(4):
+                mm_out0(1, j, ("dh", Z), True, False)
+            vec_u2(1, 0, 1)
+            for m in range(4):
+                mm_out1(Z, m)
+                copy_out1("s", Z, m)
+            q_t(H, 1)
+            vec_gate(R, 1, "s", "hh")
+            for m in range(4):
+                mm_out1(H, m)
+                copy_out1("s", H, m)
+            q_f(H, 1)
+            turn_gate(R, 1)
+            feature_tile(("F", R, 1))
+            copy_gate("s", R, 1, 0)
+            q_t(R, 1)
+            copy_gate("v", R, 1, 1)
+            q_f(R, 1, 0, 2)
+            q_f(R, 1, 1, 2)
+            for j in range(4):
+                mm_out0(1, j, (H, R), False, True)
+            for j in range(4):
+                vec_add(1, j)
+            for m in range(4):
+                mm_out1(R, m)
+                copy_out1("s" if m < 3 else "v", R, m)

@@ -51,11 +51,24 @@ def tile_gatedgraphconvolution_pb_v_kernel(
             for i in range(pieces):
                 nc.sync.dma_start(out=view[:, i * n : (i + 1) * n, :], in_=src[:, i * n : (i + 1) * n, :])
 
-        def load_act(name, g, src, pieces):
-            t = sb([P, 2048], F32, "%s%d" % (name, g))
-            act[name, g] = t
+        def act_tile(name, g, tag):
+            t = sb([P, 2048], F32, "%s%d" % (name, g), tag)
+            act[name, g] = t[:].rearrange("p (j c) -> p j c", j=4)
+            return act[name, g]
+
+        def load_gates(g, pieces):
+            t = sb([P, 4 * G], F32, "gates%d" % g)
+            view = t[:].rearrange("p (j k) -> p j k", j=4)
             n = 4 // pieces
-            view = t[:].rearrange("p (j c) -> p j c", j=4)
+            src = rows_src(gates, g)
+            for i in range(pieces):
+                nc.sync.dma_start(out=view[:, i * n : (i + 1) * n, :], in_=src[:, i * n : (i + 1) * n, :])
+            for block, name in ((Z, "z"), (R, "r"), (H, "hc")):
+                act[name, g] = view[:, :, 512 * block : 512 * (block + 1)]
+
+        def load_act(name, g, src, pieces):
+            view = act_tile(name, g, "%s%d" % (name, g))
+            n = 4 // pieces
             for i in range(pieces):
                 nc.sync.dma_start(out=view[:, i * n : (i + 1) * n, :], in_=src[:, i * n : (i + 1) * n, :])
 
@@ -141,7 +154,7 @@ def tile_gatedgraphconvolution_pb_v_kernel(
                 nc.vector.tensor_scalar_mul(out, in_, sign)
 
         def copy_out1(eng, gate, m):
-            stage = sb([P, 512], F32, "stage_%d_%d" % (gate, m), "stage", 4)
+            stage = sb([P, 512], F32, "stage_%d_%d" % (gate, m), "stage", 8)
             out = stage[:].rearrange("p (q f) -> p q f", f=4)
             in_ = banks["o1", gate, m][:].rearrange("p (f q) -> p q f", f=4)
             sign = -1.0 if gate == R else 1.0
@@ -149,7 +162,8 @@ def tile_gatedgraphconvolution_pb_v_kernel(
                 nc.scalar.activation(out=out, in_=in_, func=ACT.Copy, scale=sign)
             else:
                 nc.vector.tensor_scalar_mul(out, in_, sign)
-            nc.sync.dma_start(out=out_1[128 * m : 128 * (m + 1), 512 * gate : 512 * (gate + 1)], in_=stage[:])
+            store = nc.scalar if eng == "s" else nc.sync
+            store.dma_start(out=out_1[128 * m : 128 * (m + 1), 512 * gate : 512 * (gate + 1)], in_=stage[:])
 
         def alloc_codes(key, tag, bufs):
             nm = "_".join(str(x) for x in (key if isinstance(key, tuple) else (key,)))
@@ -167,11 +181,10 @@ def tile_gatedgraphconvolution_pb_v_kernel(
 
         def vec_e(g, j):
             if j == 0:
-                act["e", g] = sb([P, 2048], F32, "e%d" % g)
-            c = slice(512 * j, 512 * (j + 1))
+                act_tile("e", g, "e%d" % g)
             nc.vector.scalar_tensor_tensor(
-                out=act["e", g][:, c].rearrange("p (q m) -> p q m", m=4),
-                in0=act["z", g][:, c].rearrange("p (q m) -> p q m", m=4),
+                out=act["e", g][:, j, :].rearrange("p (q m) -> p q m", m=4),
+                in0=act["z", g][:, j, :].rearrange("p (q m) -> p q m", m=4),
                 scalar=1.0,
                 in1=banks["dh", g, j][:].rearrange("p (m q) -> p q m", m=4),
                 op0=SUB,
@@ -180,35 +193,34 @@ def tile_gatedgraphconvolution_pb_v_kernel(
 
         def scal_s(g, i, n):
             if i == 0:
-                act["s", g] = sb([P, 2048], F32, "s%d" % g)
-            w = 2048 // n
-            c = slice(w * i, w * (i + 1))
-            nc.scalar.activation(out=act["s", g][:, c], in_=act["hc", g][:, c], func=ACT.Square)
+                act_tile("s", g, "s%d" % g)
+            c = slice(4 // n * i, 4 // n * (i + 1))
+            nc.scalar.activation(out=act["s", g][:, c, :], in_=act["hc", g][:, c, :], func=ACT.Square)
 
         def scal_sr(g, i, n):
             if i == 0:
-                act["sr", g] = sb([P, 2048], F32, "sr%d" % g, "sr", 1)
-            w = 2048 // n
-            c = slice(w * i, w * (i + 1))
-            nc.scalar.activation(out=act["sr", g][:, c], in_=act["r", g][:, c], func=ACT.Square, bias=neg_half[:, 0:1])
+                act_tile("sr", g, "sr")
+            c = slice(4 // n * i, 4 // n * (i + 1))
+            nc.scalar.activation(out=act["sr", g][:, c, :], in_=act["r", g][:, c, :], func=ACT.Square, bias=neg_half[:, 0:1])
 
         def vec_dah(g, i, n):
-            w = 2048 // n
-            c = slice(w * i, w * (i + 1))
+            c = slice(4 // n * i, 4 // n * (i + 1))
             s = act["s", g]
-            nc.vector.scalar_tensor_tensor(out=s[:, c], in0=s[:, c], scalar=1.0, in1=act["e", g][:, c], op0=SUB, op1=MULT)
+            nc.vector.scalar_tensor_tensor(
+                out=s[:, c, :], in0=s[:, c, :], scalar=1.0, in1=act["e", g][:, c, :], op0=SUB, op1=MULT
+            )
 
         def vec_tp(g, i, n):
-            w = 2048 // n
-            c = slice(w * i, w * (i + 1))
-            hc = act["hc", g]
-            nc.vector.tensor_tensor(out=hc[:, c], in0=hc[:, c], in1=act["hn", g][:, c], op=SUB)
+            c = slice(4 // n * i, 4 // n * (i + 1))
+            hn = act["hn", g]
+            nc.vector.tensor_tensor(out=hn[:, c, :], in0=act["hc", g][:, c, :], in1=hn[:, c, :], op=SUB)
 
         def vec_u2(g, i, n):
-            w = 2048 // n
-            c = slice(w * i, w * (i + 1))
+            c = slice(4 // n * i, 4 // n * (i + 1))
             hhg = act["hh", g]
-            nc.vector.scalar_tensor_tensor(out=hhg[:, c], in0=act["sr", g][:, c], scalar=0.25, in1=hhg[:, c], op0=SUB, op1=MULT)
+            nc.vector.scalar_tensor_tensor(
+                out=hhg[:, c, :], in0=act["sr", g][:, c, :], scalar=0.25, in1=hhg[:, c, :], op0=SUB, op1=MULT
+            )
 
         def vec_gate(gate, g, a, b, i=0, n=1):
             if i == 0:
@@ -217,21 +229,20 @@ def tile_gatedgraphconvolution_pb_v_kernel(
             q = slice(w * i, w * (i + 1))
             nc.vector.tensor_tensor(
                 out=tm[gate, g][:].rearrange("p (f q t) -> p q t f", f=4, t=4)[:, q, :, :],
-                in0=act[a, g][:].rearrange("p (t q f) -> p q t f", t=4, f=4)[:, q, :, :],
-                in1=act[b, g][:].rearrange("p (t q f) -> p q t f", t=4, f=4)[:, q, :, :],
+                in0=act[a, g].rearrange("p t (q f) -> p q t f", f=4)[:, q, :, :],
+                in1=act[b, g].rearrange("p t (q f) -> p q t f", f=4)[:, q, :, :],
                 op=MULT,
             )
 
         def vec_add(g, j):
-            c = slice(512 * j, 512 * (j + 1))
-            e = act["e", g]
+            e = act["e", g][:, j, :]
             nc.vector.tensor_tensor(
-                out=e[:, c].rearrange("p (q m) -> p q m", m=4),
+                out=e.rearrange("p (q m) -> p q m", m=4),
                 in0=banks["o0", g, j][:].rearrange("p (m q) -> p q m", m=4),
-                in1=e[:, c].rearrange("p (q m) -> p q m", m=4),
+                in1=e.rearrange("p (q m) -> p q m", m=4),
                 op=ADD,
             )
-            nc.sync.dma_start(out=out_0[g].rearrange("(p j) c -> p j c", j=4)[:, j, :], in_=e[:, c])
+            nc.sync.dma_start(out=out_0[g].rearrange("(p j) c -> p j c", j=4)[:, j, :], in_=e)
 
         def interleave_h(g):
             fm["h", g] = sb([P, 2048], BF16, "fm_h_%d" % g, "fm", 4)
@@ -255,14 +266,12 @@ def tile_gatedgraphconvolution_pb_v_kernel(
             load_act("r", 0, gate_src(0, R), 1)
             load_act("hh", 0, rows_src(hh, 0), 1)
             load_raw("g1", grad_out[1].rearrange("(p j) o -> p j o", j=4), 1)
-            load_act("z", 1, gate_src(1, Z), 1)
-            load_act("hc", 1, gate_src(1, H), 1)
+            load_gates(1, 2)
             raw_u = sb([P, 4 * G], BF16, "raw_u")
             u_src = gru_U.rearrange("(p m) k -> p (m k)", m=4)
             for i in range(2):
                 nc.sync.dma_start(out=raw_u[:, 2 * G * i : 2 * G * (i + 1)], in_=u_src[:, 2 * G * i : 2 * G * (i + 1)])
             load_act("hn", 1, rows_src(hnew, 1), 1)
-            load_act("r", 1, gate_src(1, R), 1)
             load_act("hh", 1, rows_src(hh, 1), 1)
             load_raw("h0", annotations[0].rearrange("(p j) c -> p j c", j=4), 1)
             load_raw("h1", annotations[1].rearrange("(p j) c -> p j c", j=4), 1)
@@ -283,10 +292,10 @@ def tile_gatedgraphconvolution_pb_v_kernel(
             copy_rows("s", "W", 0, "W0")
             copy_rows("v", "W", 1, "W1")
             copy_rows("s", ("g", 0), 0, "g00")
-            copy_rows("v", ("g", 0), 1, "g01")
+            copy_rows("s", ("g", 0), 1, "g01")
             quant("W", fm["W"], E4M3, "W", 1)
-            quant(("g", 0), fm["g", 0], E5M2, "g0", 1, 0, 2)
-            quant(("g", 0), fm["g", 0], E5M2, "g0", 1, 1, 2)
+            for i in range(2):
+                quant(("g", 0), fm["g", 0], E5M2, "g0", 1, i, 2)
             for j in range(4):
                 mm_dhnew(0, j)
 
@@ -299,7 +308,7 @@ def tile_gatedgraphconvolution_pb_v_kernel(
             scal_sr(0, 0, 1)
             vec_tp(0, 0, 2)
             vec_tp(0, 1, 2)
-            vec_gate(Z, 0, "e", "hc")
+            vec_gate(Z, 0, "e", "hn")
             turn_gate(Z, 0)
             feature_tile(("F", Z, 0))
             copy_gate("s", Z, 0, 0)
@@ -345,7 +354,9 @@ def tile_gatedgraphconvolution_pb_v_kernel(
             for block in range(3):
                 quant(("U", block), fm["U", block], E4M3, "U%d" % block, 1)
             scal_sr(1, 0, 1)
-            vec_gate(Z, 1, "e", "hc")
+            interleave_h(0)
+            interleave_h(1)
+            vec_gate(Z, 1, "e", "hn")
             for j in range(4):
                 mm_out0(0, j, ("dh", Z, R, H), True, True)
             for j in range(4):
@@ -354,38 +365,41 @@ def tile_gatedgraphconvolution_pb_v_kernel(
             feature_tile(("F", Z, 1))
             copy_gate("s", Z, 1, 0)
             copy_gate("s", Z, 1, 1)
-            q_t(Z, 1)
-            interleave_h(0)
-            interleave_h(1)
-            vec_gate(H, 1, "s", "r")
-            turn_gate(H, 1)
-            q_f(Z, 1)
             for g in range(2):
                 quant(("h", g), fm["h", g], E4M3, "h%d" % g, 1)
+            q_t(Z, 1)
+            vec_gate(H, 1, "s", "r")
+            for m in range(4):
+                mm_out1(Z, m)
+            turn_gate(H, 1)
+            copy_out1("s", Z, 0)
+            copy_out1("s", Z, 1)
             feature_tile(("F", H, 1))
             copy_gate("s", H, 1, 0)
             copy_gate("s", H, 1, 1)
+            q_f(Z, 1)
+            copy_out1("s", Z, 2)
+            copy_out1("s", Z, 3)
+            q_t(H, 1)
+            vec_u2(1, 0, 1)
             for j in range(4):
                 mm_out0(1, j, ("dh", Z), True, False)
-            vec_u2(1, 0, 1)
-            for m in range(4):
-                mm_out1(Z, m)
-                copy_out1("s", Z, m)
-            q_t(H, 1)
-            vec_gate(R, 1, "s", "hh")
+            q_f(H, 1)
             for m in range(4):
                 mm_out1(H, m)
                 copy_out1("s", H, m)
-            q_f(H, 1)
+            vec_gate(R, 1, "s", "hh")
             turn_gate(R, 1)
+            for j in range(4):
+                mm_out0(1, j, (H,), False, False)
             feature_tile(("F", R, 1))
-            copy_gate("s", R, 1, 0)
             q_t(R, 1)
-            copy_gate("v", R, 1, 1)
+            copy_gate("v", R, 1, 0)
+            copy_gate("s", R, 1, 1)
             q_f(R, 1, 0, 2)
             q_f(R, 1, 1, 2)
             for j in range(4):
-                mm_out0(1, j, (H, R), False, True)
+                mm_out0(1, j, (R,), False, True)
             for j in range(4):
                 vec_add(1, j)
             for m in range(4):

@@ -38,11 +38,13 @@ def tile_gatedgraphconvolution_pb_v_kernel(
         ident = sb([P, P], F32, "ident")
         neg_half = sb([P, 1], F32, "neg_half")
         warm = sb([P, 1], F32, "warm")
+        zeros = sb([P, 512], BF16, "zeros", "stage", 8)
 
         raw, fm, tm = {}, {}, {}
         codes, scales = {}, {}
         act = {}
         banks = {}
+        stages = {}
 
         def load_raw(name, src, pieces):
             raw[name] = sb([P, 2048], BF16, "raw_" + name, "raw", 3)
@@ -56,15 +58,16 @@ def tile_gatedgraphconvolution_pb_v_kernel(
             act[name, g] = t[:].rearrange("p (j c) -> p j c", j=4)
             return act[name, g]
 
-        def load_gates(g, pieces):
-            t = sb([P, 4 * G], F32, "gates%d" % g)
+        def load_gates(g, blocks, pieces):
+            w = 512 * len(blocks)
+            t = sb([P, 4 * w], F32, "gates%d%d" % (g, blocks[0]))
             view = t[:].rearrange("p (j k) -> p j k", j=4)
             n = 4 // pieces
-            src = rows_src(gates, g)
+            src = rows_src(gates, g)[:, :, 512 * blocks[0] : 512 * blocks[0] + w]
             for i in range(pieces):
                 nc.sync.dma_start(out=view[:, i * n : (i + 1) * n, :], in_=src[:, i * n : (i + 1) * n, :])
-            for block, name in ((Z, "z"), (R, "r"), (H, "hc")):
-                act[name, g] = view[:, :, 512 * block : 512 * (block + 1)]
+            for k, block in enumerate(blocks):
+                act["z" if block == Z else "r" if block == R else "hc", g] = view[:, :, 512 * k : 512 * (k + 1)]
 
         def load_act(name, g, src, pieces):
             view = act_tile(name, g, "%s%d" % (name, g))
@@ -88,13 +91,22 @@ def tile_gatedgraphconvolution_pb_v_kernel(
                 for u in range(2):
                     turn(b[:, 256 * i + 128 * u : 256 * i + 128 * (u + 1)], words, base, u)
 
+        def dummies(n):
+            b = bank("dummy")
+            for i in range(n):
+                nc.tensor.matmul(b[:], lhsT=zeros[:, 0:128], rhs=zeros[:], start=True, stop=True)
+
         def turn_gate(gate, g):
             words = tm[gate, g][:].bitcast(F32)
             for u in range(2):
                 b = bank("tf_%d_%d_%d" % (gate, g, u))
                 banks["f", gate, g, u] = b
                 for f in range(4):
-                    turn(b[:, 128 * f : 128 * (f + 1)], words, 256 * f, u)
+                    dst = b[:, 128 * f : 128 * (f + 1)]
+                    if gate == R:
+                        turn(dst, words, 256 * f, u)
+                    else:
+                        nc.tensor.transpose(dst, words[:, 2 * f + u : 1024 : 8], ident[:])
 
         def mx(out, lhs, lcols, lfmt, rhs, rfmt, start, stop):
             nc.tensor.matmul_mx(
@@ -155,15 +167,23 @@ def tile_gatedgraphconvolution_pb_v_kernel(
 
         def copy_out1(eng, gate, m):
             stage = sb([P, 512], F32, "stage_%d_%d" % (gate, m), "stage", 8)
-            out = stage[:].rearrange("p (q f) -> p q f", f=4)
-            in_ = banks["o1", gate, m][:].rearrange("p (f q) -> p q f", f=4)
+            out = stage[:]
+            in_ = banks["o1", gate, m][:]
+            if gate == R:
+                out = out.rearrange("p (q f) -> p q f", f=4)
+                in_ = in_.rearrange("p (f q) -> p q f", f=4)
             sign = -1.0 if gate == R else 1.0
             if eng == "s":
                 nc.scalar.activation(out=out, in_=in_, func=ACT.Copy, scale=sign)
             else:
                 nc.vector.tensor_scalar_mul(out, in_, sign)
-            store = nc.scalar if eng == "s" else nc.sync
-            store.dma_start(out=out_1[128 * m : 128 * (m + 1), 512 * gate : 512 * (gate + 1)], in_=stage[:])
+            stages[gate, m] = stage
+
+        def store_out1(gate, *ms):
+            for m in ms:
+                nc.sync.dma_start(
+                    out=out_1[128 * m : 128 * (m + 1), 512 * gate : 512 * (gate + 1)], in_=stages[gate, m][:]
+                )
 
         def alloc_codes(key, tag, bufs):
             nm = "_".join(str(x) for x in (key if isinstance(key, tuple) else (key,)))
@@ -228,7 +248,7 @@ def tile_gatedgraphconvolution_pb_v_kernel(
             w = 128 // n
             q = slice(w * i, w * (i + 1))
             nc.vector.tensor_tensor(
-                out=tm[gate, g][:].rearrange("p (f q t) -> p q t f", f=4, t=4)[:, q, :, :],
+                out=tm[gate, g][:].rearrange("p (f q t) -> p q t f" if gate == R else "p (q f t) -> p q t f", f=4, t=4)[:, q, :, :],
                 in0=act[a, g].rearrange("p t (q f) -> p q t f", f=4)[:, q, :, :],
                 in1=act[b, g].rearrange("p t (q f) -> p q t f", f=4)[:, q, :, :],
                 op=MULT,
@@ -242,7 +262,10 @@ def tile_gatedgraphconvolution_pb_v_kernel(
                 in1=e.rearrange("p (q m) -> p q m", m=4),
                 op=ADD,
             )
-            nc.sync.dma_start(out=out_0[g].rearrange("(p j) c -> p j c", j=4)[:, j, :], in_=e)
+
+        def store_out0(g, first, last):
+            rows = out_0[g].rearrange("(p j) c -> p j c", j=4)
+            nc.sync.dma_start(out=rows[:, first:last, :], in_=act["e", g][:, first:last, :])
 
         def interleave_h(g):
             fm["h", g] = sb([P, 2048], BF16, "fm_h_%d" % g, "fm", 4)
@@ -258,28 +281,30 @@ def tile_gatedgraphconvolution_pb_v_kernel(
             quant(("F", gate, g), fm["F", gate, g], E5M2, "F", 4, part, parts)
 
         with tc.manual_schedule():
-            load_raw("W", dense_W.rearrange("(p m) o -> p m o", m=4), 2)
-            load_raw("g0", grad_out[0].rearrange("(p j) o -> p j o", j=4), 2)
-            load_act("z", 0, gate_src(0, Z), 2)
-            load_act("hc", 0, gate_src(0, H), 2)
-            load_act("hn", 0, rows_src(hnew, 0), 2)
-            load_act("r", 0, gate_src(0, R), 1)
-            load_act("hh", 0, rows_src(hh, 0), 1)
-            load_raw("g1", grad_out[1].rearrange("(p j) o -> p j o", j=4), 1)
-            load_gates(1, 2)
             raw_u = sb([P, 4 * G], BF16, "raw_u")
             u_src = gru_U.rearrange("(p m) k -> p (m k)", m=4)
+            load_raw("W", dense_W.rearrange("(p m) o -> p m o", m=4), 2)
+            load_raw("g0", grad_out[0].rearrange("(p j) o -> p j o", j=4), 2)
+            load_gates(0, (Z,), 2)
+            load_gates(0, (H,), 2)
+            load_act("hn", 0, rows_src(hnew, 0), 2)
+            load_raw("h0", annotations[0].rearrange("(p j) c -> p j c", j=4), 1)
+            load_gates(0, (R,), 1)
+            load_act("hh", 0, rows_src(hh, 0), 1)
+            load_raw("g1", grad_out[1].rearrange("(p j) o -> p j o", j=4), 1)
+            load_gates(1, (Z, R, H), 2)
+            load_act("hn", 1, rows_src(hnew, 1), 1)
             for i in range(2):
                 nc.sync.dma_start(out=raw_u[:, 2 * G * i : 2 * G * (i + 1)], in_=u_src[:, 2 * G * i : 2 * G * (i + 1)])
-            load_act("hn", 1, rows_src(hnew, 1), 1)
-            load_act("hh", 1, rows_src(hh, 1), 1)
-            load_raw("h0", annotations[0].rearrange("(p j) c -> p j c", j=4), 1)
             load_raw("h1", annotations[1].rearrange("(p j) c -> p j c", j=4), 1)
+            load_act("hh", 1, rows_src(hh, 1), 1)
 
             nc.vector.memset(neg_half[:], -0.5)
             nc.vector.memset(warm[:], 0.0)
             nc.scalar.activation(out=warm[:], in_=warm[:], func=ACT.Square)
             make_identity(nc, ident[:])
+            nc.vector.memset(zeros[:], 0.0)
+            dummies(5)
 
             w_words = raw["W"][:].bitcast(F32)
             g0_words = raw["g0"][:].bitcast(F32)
@@ -305,6 +330,7 @@ def tile_gatedgraphconvolution_pb_v_kernel(
                 vec_e(0, j)
             vec_dah(0, 0, 2)
             vec_dah(0, 1, 2)
+            interleave_h(0)
             scal_sr(0, 0, 1)
             vec_tp(0, 0, 2)
             vec_tp(0, 1, 2)
@@ -340,7 +366,9 @@ def tile_gatedgraphconvolution_pb_v_kernel(
             feature_tile(("F", R, 0))
             copy_gate("s", R, 0, 0)
             copy_gate("s", R, 0, 1)
-            vec_dah(1, 0, 1)
+            vec_tp(1, 0, 1)
+            q_f(R, 0)
+            vec_gate(Z, 1, "e", "hn")
             u_words = raw_u[:].bitcast(F32)
             for block in range(3):
                 feature_tile(("U", block))
@@ -349,59 +377,66 @@ def tile_gatedgraphconvolution_pb_v_kernel(
                         "U%d%d" % (block, i), u_words, (768 * 2 * i + 256 * block, 768 * (2 * i + 1) + 256 * block)
                     )
                     copy_rows("s", ("U", block), i, "U%d%d" % (block, i))
-            q_f(R, 0)
-            vec_tp(1, 0, 1)
-            for block in range(3):
-                quant(("U", block), fm["U", block], E4M3, "U%d" % block, 1)
-            scal_sr(1, 0, 1)
-            interleave_h(0)
-            interleave_h(1)
-            vec_gate(Z, 1, "e", "hn")
-            for j in range(4):
-                mm_out0(0, j, ("dh", Z, R, H), True, True)
-            for j in range(4):
-                vec_add(0, j)
             turn_gate(Z, 1)
+            quant(("U", 0), fm["U", 0], E4M3, "U0", 1)
+            vec_dah(1, 0, 1)
+            for block in range(1, 3):
+                quant(("U", block), fm["U", block], E4M3, "U%d" % block, 1)
             feature_tile(("F", Z, 1))
             copy_gate("s", Z, 1, 0)
             copy_gate("s", Z, 1, 1)
-            for g in range(2):
-                quant(("h", g), fm["h", g], E4M3, "h%d" % g, 1)
+            interleave_h(1)
+            scal_sr(1, 0, 1)
             q_t(Z, 1)
             vec_gate(H, 1, "s", "r")
-            for m in range(4):
-                mm_out1(Z, m)
+            for j in range(4):
+                mm_out0(0, j, ("dh", Z, R, H), True, True)
+            quant(("h", 0), fm["h", 0], E4M3, "h0", 1)
+            quant(("h", 1), fm["h", 1], E4M3, "h1", 1)
+            q_f(Z, 1)
+            vec_add(0, 0)
+            vec_add(0, 1)
+            store_out0(0, 0, 2)
             turn_gate(H, 1)
-            copy_out1("s", Z, 0)
-            copy_out1("s", Z, 1)
+            q_t(H, 1)
             feature_tile(("F", H, 1))
             copy_gate("s", H, 1, 0)
             copy_gate("s", H, 1, 1)
-            q_f(Z, 1)
-            copy_out1("s", Z, 2)
-            copy_out1("s", Z, 3)
-            q_t(H, 1)
             vec_u2(1, 0, 1)
-            for j in range(4):
-                mm_out0(1, j, ("dh", Z), True, False)
+            for m in range(4):
+                mm_out1(Z, m)
+                copy_out1("s", Z, m)
+                store_out1(Z, m)
             q_f(H, 1)
+            vec_gate(R, 1, "s", "hh")
             for m in range(4):
                 mm_out1(H, m)
                 copy_out1("s", H, m)
-            vec_gate(R, 1, "s", "hh")
-            turn_gate(R, 1)
+                store_out1(H, m)
             for j in range(4):
-                mm_out0(1, j, (H,), False, False)
+                mm_out0(1, j, ("dh", Z), True, False)
+            turn_gate(R, 1)
             feature_tile(("F", R, 1))
+            vec_add(0, 2)
             q_t(R, 1)
+            vec_add(0, 3)
+            store_out0(0, 2, 4)
             copy_gate("v", R, 1, 0)
             copy_gate("s", R, 1, 1)
+            for m in range(2):
+                mm_out1(R, m)
+                copy_out1("s", R, m)
+                store_out1(R, m)
+            for j in range(4):
+                mm_out0(1, j, (H,), False, False)
             q_f(R, 1, 0, 2)
             q_f(R, 1, 1, 2)
             for j in range(4):
                 mm_out0(1, j, (R,), False, True)
             for j in range(4):
                 vec_add(1, j)
-            for m in range(4):
+                store_out0(1, j, j + 1)
+            for m in (2, 3,):
                 mm_out1(R, m)
                 copy_out1("s" if m < 3 else "v", R, m)
+                store_out1(R, m)

from contextlib import ExitStack

import concourse.mybir as mybir
from concourse.masks import make_identity

NODES, GROUP, C, O, G = 1024, 512, 512, 512, 1536
P = 128
FLOPS = 2 * NODES * C * O + 4 * NODES * C * G
BYTES = 2 * (NODES * O + C * O + C * G + NODES * C) + 4 * (NODES * G + 2 * NODES * C) + 4 * (NODES * C + C * G)

F32 = mybir.dt.float32
BF16 = mybir.dt.bfloat16
U32 = mybir.dt.uint32
U8 = mybir.dt.uint8
E4M3 = mybir.dt.float8_e4m3fn_x4
E5M2 = mybir.dt.float8_e5m2_x4
ADD = mybir.AluOpType.add
SUB = mybir.AluOpType.subtract
MULT = mybir.AluOpType.mult
ACT = mybir.ActivationFunctionType
Z, R, H = 0, 1, 2


def tile_gatedgraphconvolution_pb_v_kernel(
    tc, gx, annotations, gru_U, gru_b_h, dense_W, dense_b, gates, hh, hnew, grad_out, out_0, out_1
):
    nc = tc.nc
    with ExitStack() as ctx:
        pool = ctx.enter_context(tc.tile_pool(name="pool", bufs=1))
        psum = ctx.enter_context(tc.psum_pool(name="psum", bufs=8))

        def sb(shape, dtype, name, tag=None, bufs=1):
            return pool.tile(shape, dtype, name=name, tag=tag or name, bufs=bufs, align_bytes=64)

        def bank(name):
            return psum.tile([P, 512], F32, name=name, tag="bank", bufs=8)

        ident = sb([P, P], F32, "ident")
        neg_half = sb([P, 1], F32, "neg_half")
        warm = sb([P, 1], F32, "warm")
        zeros = sb([P, 512], BF16, "zeros", "stage", 8)

        raw, fm, tm = {}, {}, {}
        codes, scales = {}, {}
        act = {}
        banks = {}
        stages = {}

        def load_raw(name, src, pieces):
            raw[name] = sb([P, 2048], BF16, "raw_" + name, "raw", 3)
            n = 4 // pieces
            view = raw[name][:].rearrange("p (j c) -> p j c", j=4)
            for i in range(pieces):
                nc.sync.dma_start(out=view[:, i * n : (i + 1) * n, :], in_=src[:, i * n : (i + 1) * n, :])

        def act_tile(name, g, tag):
            t = sb([P, 2048], F32, "%s%d" % (name, g), tag)
            act[name, g] = t[:].rearrange("p (j c) -> p j c", j=4)
            return act[name, g]

        def load_gates(g, blocks, pieces):
            w = 512 * len(blocks)
            t = sb([P, 4 * w], F32, "gates%d%d" % (g, blocks[0]))
            view = t[:].rearrange("p (j k) -> p j k", j=4)
            n = 4 // pieces
            src = rows_src(gates, g)[:, :, 512 * blocks[0] : 512 * blocks[0] + w]
            for i in range(pieces):
                nc.sync.dma_start(out=view[:, i * n : (i + 1) * n, :], in_=src[:, i * n : (i + 1) * n, :])
            for k, block in enumerate(blocks):
                act["z" if block == Z else "r" if block == R else "hc", g] = view[:, :, 512 * k : 512 * (k + 1)]

        def load_act(name, g, src, pieces):
            view = act_tile(name, g, "%s%d" % (name, g))
            n = 4 // pieces
            for i in range(pieces):
                nc.sync.dma_start(out=view[:, i * n : (i + 1) * n, :], in_=src[:, i * n : (i + 1) * n, :])

        def gate_src(g, block):
            return gates[GROUP * g : GROUP * (g + 1), 512 * block : 512 * (block + 1)].rearrange("(p j) c -> p j c", j=4)

        def rows_src(x, g):
            return x[GROUP * g : GROUP * (g + 1), :].rearrange("(p j) c -> p j c", j=4)

        def turn(dst, words, base, u):
            nc.tensor.transpose(dst, words[:, base + u : base + 256 : 2], ident[:])

        def turn_rows(key, words, bases):
            b = bank("tr_%s" % key)
            banks[key] = b
            for i, base in enumerate(bases):
                for u in range(2):
                    turn(b[:, 256 * i + 128 * u : 256 * i + 128 * (u + 1)], words, base, u)

        def dummies(n):
            b = bank("dummy")
            for i in range(n):
                nc.tensor.matmul(b[:], lhsT=zeros[:, 0:128], rhs=zeros[:], start=True, stop=True)

        def turn_gate(gate, g):
            words = tm[gate, g][:].bitcast(F32)
            for u in range(2):
                b = bank("tf_%d_%d_%d" % (gate, g, u))
                banks["f", gate, g, u] = b
                for f in range(4):
                    dst = b[:, 128 * f : 128 * (f + 1)]
                    if gate == R:
                        turn(dst, words, 256 * f, u)
                    else:
                        nc.tensor.transpose(dst, words[:, 2 * f + u : 1024 : 8], ident[:])

        def mx(out, lhs, lcols, lfmt, rhs, rfmt, start, stop):
            nc.tensor.matmul_mx(
                out=out[:],
                lhsT=codes[lhs][:, lcols].bitcast(lfmt),
                lhsT_scale=scales[lhs][:, lcols],
                rhs=codes[rhs][:].bitcast(rfmt),
                rhs_scale=scales[rhs][:],
                start=start,
                stop=stop,
            )

        def cols(i):
            return slice(128 * i, 128 * (i + 1))

        def mm_dhnew(g, j):
            b = bank("dh_%d_%d" % (g, j))
            banks["dh", g, j] = b
            mx(b, ("g", g), cols(j), E5M2, "W", E4M3, True, True)

        def mm_out0(g, j, parts, start, stop):
            if start:
                banks["o0", g, j] = bank("o0_%d_%d" % (g, j))
            b = banks["o0", g, j]
            for i, part in enumerate(parts):
                st = start and i == 0
                sp = stop and i == len(parts) - 1
                if part == "dh":
                    mx(b, ("g", g), cols(j), E5M2, "W", E4M3, st, sp)
                else:
                    mx(b, ("F", part, g), cols(j), E5M2, ("U", part), E4M3, st, sp)

        def mm_out1(gate, m):
            b = bank("o1_%d_%d" % (gate, m))
            banks["o1", gate, m] = b
            for g in range(2):
                mx(b, ("h", g), cols(m), E4M3, ("T", gate, g), E5M2, g == 0, g == 1)

        def feature_tile(key):
            fm[key] = sb([P, 2048], BF16, "fm_%s" % "_".join(str(x) for x in (key if isinstance(key, tuple) else (key,))), "fm", 4)

        def copy_rows(eng, key, half, bank_key):
            out = fm[key][:].bitcast(F32)[:, 512 * half : 512 * (half + 1)].rearrange("q (m p u) -> q m p u", m=2, u=2)
            in_ = banks[bank_key][:].rearrange("q (m u p) -> q m p u", m=2, u=2)
            if eng == "s":
                nc.scalar.copy(out=out, in_=in_)
            else:
                nc.vector.tensor_copy(out=out, in_=in_)

        def copy_gate(eng, gate, g, u):
            out = fm["F", gate, g][:, 1024 * u : 1024 * (u + 1)].rearrange("q (e p f) -> q e p f", e=2, f=4)
            in_ = banks["f", gate, g, u][:].bitcast(BF16).rearrange("q (f p e) -> q e p f", f=4, e=2)
            sign = -1.0 if gate == R else 1.0
            if eng == "s":
                nc.scalar.activation(out=out, in_=in_, func=ACT.Copy, scale=sign)
            else:
                nc.vector.tensor_scalar_mul(out, in_, sign)

        def copy_out1(eng, gate, m):
            stage = sb([P, 512], F32, "stage_%d_%d" % (gate, m), "stage", 8)
            out = stage[:]
            in_ = banks["o1", gate, m][:]
            if gate == R:
                out = out.rearrange("p (q f) -> p q f", f=4)
                in_ = in_.rearrange("p (f q) -> p q f", f=4)
            sign = -1.0 if gate == R else 1.0
            if eng == "s":
                nc.scalar.activation(out=out, in_=in_, func=ACT.Copy, scale=sign)
            else:
                nc.vector.tensor_scalar_mul(out, in_, sign)
            stages[gate, m] = stage

        def store_out1(gate, *ms):
            for m in ms:
                nc.sync.dma_start(
                    out=out_1[128 * m : 128 * (m + 1), 512 * gate : 512 * (gate + 1)], in_=stages[gate, m][:]
                )

        def alloc_codes(key, tag, bufs):
            nm = "_".join(str(x) for x in (key if isinstance(key, tuple) else (key,)))
            codes[key] = sb([P, 512], U32, "c_" + nm, "c_" + tag, bufs)
            scales[key] = sb([P, 512], U8, "s_" + nm, "s_" + tag, bufs)

        def quant(key, src, fmt, tag, bufs, part=0, parts=1):
            if part == 0:
                alloc_codes(key, tag, bufs)
            w = 512 // parts
            c = slice(w * part, w * (part + 1))
            nc.vector.quantize_mx(
                out=codes[key][:, c].bitcast(fmt), scales=scales[key][:, c], in_=src[:, 4 * w * part : 4 * w * (part + 1)]
            )

        def vec_e(g, j):
            if j == 0:
                act_tile("e", g, "e%d" % g)
            nc.vector.scalar_tensor_tensor(
                out=act["e", g][:, j, :].rearrange("p (q m) -> p q m", m=4),
                in0=act["z", g][:, j, :].rearrange("p (q m) -> p q m", m=4),
                scalar=1.0,
                in1=banks["dh", g, j][:].rearrange("p (m q) -> p q m", m=4),
                op0=SUB,
                op1=MULT,
            )

        def scal_s(g, i, n):
            if i == 0:
                act_tile("s", g, "s%d" % g)
            c = slice(4 // n * i, 4 // n * (i + 1))
            nc.scalar.activation(out=act["s", g][:, c, :], in_=act["hc", g][:, c, :], func=ACT.Square)

        def scal_sr(g, i, n):
            if i == 0:
                act_tile("sr", g, "sr")
            c = slice(4 // n * i, 4 // n * (i + 1))
            nc.scalar.activation(out=act["sr", g][:, c, :], in_=act["r", g][:, c, :], func=ACT.Square, bias=neg_half[:, 0:1])

        def vec_dah(g, i, n):
            c = slice(4 // n * i, 4 // n * (i + 1))
            s = act["s", g]
            nc.vector.scalar_tensor_tensor(
                out=s[:, c, :], in0=s[:, c, :], scalar=1.0, in1=act["e", g][:, c, :], op0=SUB, op1=MULT
            )

        def vec_tp(g, i, n):
            c = slice(4 // n * i, 4 // n * (i + 1))
            hn = act["hn", g]
            nc.vector.tensor_tensor(out=hn[:, c, :], in0=act["hc", g][:, c, :], in1=hn[:, c, :], op=SUB)

        def vec_u2(g, i, n):
            c = slice(4 // n * i, 4 // n * (i + 1))
            hhg = act["hh", g]
            nc.vector.scalar_tensor_tensor(
                out=hhg[:, c, :], in0=act["sr", g][:, c, :], scalar=0.25, in1=hhg[:, c, :], op0=SUB, op1=MULT
            )

        def vec_gate(gate, g, a, b, i=0, n=1):
            if i == 0:
                tm[gate, g] = sb([P, 2048], BF16, "tm_%d_%d" % (gate, g), "tm", 4)
            w = 128 // n
            q = slice(w * i, w * (i + 1))
            nc.vector.tensor_tensor(
                out=tm[gate, g][:].rearrange("p (f q t) -> p q t f" if gate == R else "p (q f t) -> p q t f", f=4, t=4)[:, q, :, :],
                in0=act[a, g].rearrange("p t (q f) -> p q t f", f=4)[:, q, :, :],
                in1=act[b, g].rearrange("p t (q f) -> p q t f", f=4)[:, q, :, :],
                op=MULT,
            )

        def vec_add(g, j):
            e = act["e", g][:, j, :]
            nc.vector.tensor_tensor(
                out=e.rearrange("p (q m) -> p q m", m=4),
                in0=banks["o0", g, j][:].rearrange("p (m q) -> p q m", m=4),
                in1=e.rearrange("p (q m) -> p q m", m=4),
                op=ADD,
            )

        def store_out0(g, first, last):
            rows = out_0[g].rearrange("(p j) c -> p j c", j=4)
            nc.sync.dma_start(out=rows[:, first:last, :], in_=act["e", g][:, first:last, :])

        def interleave_h(g):
            fm["h", g] = sb([P, 2048], BF16, "fm_h_%d" % g, "fm", 4)
            nc.scalar.copy(
                out=fm["h", g][:].rearrange("p (c i t) -> p c t i", i=4, t=4),
                in_=raw["h%d" % g][:].rearrange("p (t c i) -> p c t i", t=4, i=4),
            )

        def q_t(gate, g):
            quant(("T", gate, g), tm[gate, g], E5M2, "T%d%d" % (gate, g), 1)

        def q_f(gate, g, part=0, parts=1):
            quant(("F", gate, g), fm["F", gate, g], E5M2, "F", 4, part, parts)

        with tc.manual_schedule():
            raw_u = sb([P, 4 * G], BF16, "raw_u")
            u_src = gru_U.rearrange("(p m) k -> p (m k)", m=4)
            load_raw("W", dense_W.rearrange("(p m) o -> p m o", m=4), 2)
            load_raw("g0", grad_out[0].rearrange("(p j) o -> p j o", j=4), 2)
            load_gates(0, (Z,), 2)
            load_gates(0, (H,), 2)
            load_act("hn", 0, rows_src(hnew, 0), 2)
            load_raw("h0", annotations[0].rearrange("(p j) c -> p j c", j=4), 1)
            load_gates(0, (R,), 1)
            load_act("hh", 0, rows_src(hh, 0), 1)
            load_raw("g1", grad_out[1].rearrange("(p j) o -> p j o", j=4), 1)
            load_gates(1, (Z, R, H), 2)
            load_act("hn", 1, rows_src(hnew, 1), 1)
            for i in range(2):
                nc.sync.dma_start(out=raw_u[:, 2 * G * i : 2 * G * (i + 1)], in_=u_src[:, 2 * G * i : 2 * G * (i + 1)])
            load_raw("h1", annotations[1].rearrange("(p j) c -> p j c", j=4), 1)
            load_act("hh", 1, rows_src(hh, 1), 1)

            nc.vector.memset(neg_half[:], -0.5)
            nc.vector.memset(warm[:], 0.0)
            nc.scalar.activation(out=warm[:], in_=warm[:], func=ACT.Square)
            make_identity(nc, ident[:])
            nc.vector.memset(zeros[:], 0.0)
            dummies(5)

            w_words = raw["W"][:].bitcast(F32)
            g0_words = raw["g0"][:].bitcast(F32)
            feature_tile("W")
            feature_tile(("g", 0))
            for i in range(2):
                turn_rows("W%d" % i, w_words, (512 * i, 512 * i + 256))
            for i in range(2):
                turn_rows("g0%d" % i, g0_words, (512 * i, 512 * i + 256))
            copy_rows("s", "W", 0, "W0")
            copy_rows("v", "W", 1, "W1")
            copy_rows("s", ("g", 0), 0, "g00")
            copy_rows("s", ("g", 0), 1, "g01")
            quant("W", fm["W"], E4M3, "W", 1)
            for i in range(2):
                quant(("g", 0), fm["g", 0], E5M2, "g0", 1, i, 2)
            for j in range(4):
                mm_dhnew(0, j)

            scal_s(0, 0, 2)
            scal_s(0, 1, 2)
            for j in range(4):
                vec_e(0, j)
            vec_dah(0, 0, 2)
            vec_dah(0, 1, 2)
            interleave_h(0)
            scal_sr(0, 0, 1)
            vec_tp(0, 0, 2)
            vec_tp(0, 1, 2)
            vec_gate(Z, 0, "e", "hn")
            turn_gate(Z, 0)
            feature_tile(("F", Z, 0))
            copy_gate("s", Z, 0, 0)
            copy_gate("s", Z, 0, 1)
            vec_gate(H, 0, "s", "r")
            feature_tile(("g", 1))
            g1_words = raw["g1"][:].bitcast(F32)
            for i in range(2):
                turn_rows("g1%d" % i, g1_words, (512 * i, 512 * i + 256))
                copy_rows("s", ("g", 1), i, "g1%d" % i)
            q_t(Z, 0)
            vec_u2(0, 0, 1)
            turn_gate(H, 0)
            feature_tile(("F", H, 0))
            copy_gate("s", H, 0, 0)
            copy_gate("s", H, 0, 1)
            quant(("g", 1), fm["g", 1], E5M2, "g1", 1)
            q_f(Z, 0)
            for j in range(4):
                mm_dhnew(1, j)
            vec_gate(R, 0, "s", "hh")
            scal_s(1, 0, 1)
            q_t(H, 0)
            for j in range(4):
                vec_e(1, j)
            q_f(H, 0)
            q_t(R, 0)
            turn_gate(R, 0)
            feature_tile(("F", R, 0))
            copy_gate("s", R, 0, 0)
            copy_gate("s", R, 0, 1)
            vec_tp(1, 0, 1)
            q_f(R, 0)
            vec_gate(Z, 1, "e", "hn")
            u_words = raw_u[:].bitcast(F32)
            for block in range(3):
                feature_tile(("U", block))
                for i in range(2):
                    turn_rows(
                        "U%d%d" % (block, i), u_words, (768 * 2 * i + 256 * block, 768 * (2 * i + 1) + 256 * block)
                    )
                    copy_rows("s", ("U", block), i, "U%d%d" % (block, i))
            turn_gate(Z, 1)
            quant(("U", 0), fm["U", 0], E4M3, "U0", 1)
            vec_dah(1, 0, 1)
            for block in range(1, 3):
                quant(("U", block), fm["U", block], E4M3, "U%d" % block, 1)
            feature_tile(("F", Z, 1))
            copy_gate("s", Z, 1, 0)
            copy_gate("s", Z, 1, 1)
            interleave_h(1)
            scal_sr(1, 0, 1)
            q_t(Z, 1)
            vec_gate(H, 1, "s", "r")
            for j in range(4):
                mm_out0(0, j, ("dh", Z, R, H), True, True)
            quant(("h", 0), fm["h", 0], E4M3, "h0", 1)
            quant(("h", 1), fm["h", 1], E4M3, "h1", 1)
            q_f(Z, 1)
            vec_add(0, 0)
            vec_add(0, 1)
            store_out0(0, 0, 2)
            turn_gate(H, 1)
            q_t(H, 1)
            feature_tile(("F", H, 1))
            copy_gate("s", H, 1, 0)
            copy_gate("s", H, 1, 1)
            vec_u2(1, 0, 1)
            for m in range(4):
                mm_out1(Z, m)
                copy_out1("s", Z, m)
                store_out1(Z, m)
            q_f(H, 1)
            vec_gate(R, 1, "s", "hh")
            for m in range(4):
                mm_out1(H, m)
                copy_out1("s", H, m)
                store_out1(H, m)
            for j in range(4):
                mm_out0(1, j, ("dh", Z), True, False)
            turn_gate(R, 1)
            feature_tile(("F", R, 1))
            vec_add(0, 2)
            q_t(R, 1)
            vec_add(0, 3)
            store_out0(0, 2, 4)
            copy_gate("v", R, 1, 0)
            copy_gate("s", R, 1, 1)
            for m in range(2):
                mm_out1(R, m)
                copy_out1("s", R, m)
                store_out1(R, m)
            for j in range(4):
                mm_out0(1, j, (H,), False, False)
            q_f(R, 1, 0, 2)
            q_f(R, 1, 1, 2)
            for j in range(4):
                mm_out0(1, j, (R,), False, True)
            for j in range(4):
                vec_add(1, j)
                store_out0(1, j, j + 1)
            for m in (2, 3,):
                mm_out1(R, m)
                copy_out1("s" if m < 3 else "v", R, m)
                store_out1(R, m)
